import numpy as np
import ml_dtypes


def mxq(x, axis, fmt="e4m3"):
    dtype, down = {"e4m3": (ml_dtypes.float8_e4m3fn, 7), "e5m2": (ml_dtypes.float8_e5m2, 14)}[fmt]
    v = np.moveaxis(np.asarray(x, np.float32).astype(ml_dtypes.bfloat16).astype(np.float64), axis, -1)
    blocks = v.reshape(v.shape[:-1] + (-1, 32))
    amax = np.abs(blocks).max(-1, keepdims=True)
    byte = np.maximum(np.where(amax > 0, np.frexp(amax)[1] - 1 + 127, 0) - down, 1)
    scale = np.exp2(byte - 127.0)
    codes = (blocks / scale).astype(np.float32).astype(dtype).astype(np.float64)
    return np.moveaxis((codes * scale).reshape(v.shape), -1, axis)


WIDE = False


def mx_kscale(k):
    if not WIDE:
        return np.ones(k)
    levels = np.array([10, -10, 5, -5, 0])
    if k % 512:
        return np.exp2(np.random.permutation(np.resize(levels, k // 32))).repeat(32)
    a = np.empty((k // 512, 16))
    for p in range(k // 512):
        a[p, :8] = np.random.permutation(np.resize(levels, 8))
        for g in range(8):
            far = levels[np.abs(levels - a[p, g]) >= 10]
            a[p, g + 8] = far[np.random.randint(len(far))]
    return np.exp2(a.ravel()).repeat(32)


BF16 = ml_dtypes.bfloat16


def bf(x):
    return np.asarray(x, np.float32).astype(BF16)


def f64(x):
    return np.asarray(x).astype(np.float64)


N_FFT, B, T = 1024, 16, 128
STRIDE = N_FFT + 1
L = T * STRIDE


def _fourier_kernels(n_fft):
    s = np.arange(n_fft, dtype=np.float64)
    k = np.arange(n_fft, dtype=np.float64)[:, None]
    ang = 2.0 * np.pi * k * s / n_fft
    return np.sin(ang), np.cos(ang)


def draw0():
    s = mx_kscale(N_FFT)
    sx = np.concatenate([s, np.ones(1)])
    x = (np.random.standard_normal((1, B, T, STRIDE)) * sx).reshape(1, B, L)
    ws, wc = _fourier_kernels(N_FFT)
    wsin = (ws + 0.5 * np.random.standard_normal((N_FFT, N_FFT))) / np.sqrt(N_FFT) / s[None, :]
    wcos = (wc + 0.5 * np.random.standard_normal((N_FFT, N_FFT))) / np.sqrt(N_FFT) / s[None, :]
    return {"x": bf(x), "wsin": bf(wsin), "wcos": bf(wcos)}


def core(x, wsin, wcos):
    sig = f64(x)[0]
    frames = sig.reshape(B, T, STRIDE)[..., :N_FFT]
    fq = mxq(frames, 2, "e4m3")
    real = np.einsum('btn,kn->tbk', fq, mxq(f64(wcos), 1, "e4m3"))
    imag = np.einsum('btn,kn->tbk', fq, mxq(f64(wsin), 1, "e4m3"))
    return real, -imag


def e4m3fn_bytes(y):
    return np.clip(np.asarray(y, np.float64), -448.0, 448.0).astype(np.float32).astype(ml_dtypes.float8_e4m3fn).view(np.uint8)


def e4m3fn_values(b):
    return np.asarray(b, np.uint8).view(ml_dtypes.float8_e4m3fn).astype(np.float64)


def setup_inputs():
    d = draw0()
    x0 = np.asarray(d['x']).astype(np.float64)
    s = (np.max(np.abs(x0), axis=(0, 1), keepdims=True) / 448.0).astype(np.float32)
    out = {}
    for k, v in d.items():
        if k == 'x':
            out['x_bytes'] = e4m3fn_bytes(x0 / s.astype(np.float64))
            out['x_scale'] = s
        else:
            out[k] = v
    return out


def reference(x_bytes, x_scale, wsin, wcos):
    return core(e4m3fn_values(x_bytes) * x_scale.astype(np.float64), wsin, wcos)

@@ -1,0 +1,244 @@
+from contextlib import ExitStack
+
+import concourse.mybir as mybir
+from concourse.masks import make_identity
+
+FLOPS = 2 * 2048 * 1024 * 2048
+
+F32 = mybir.dt.float32
+BF16 = mybir.dt.bfloat16
+U32 = mybir.dt.uint32
+U8 = mybir.dt.uint8
+FP8 = mybir.dt.float8_e4m3fn
+FP8X4 = mybir.dt.float8_e4m3fn_x4
+MULT = mybir.AluOpType.mult
+COPY = mybir.ActivationFunctionType.Copy
+
+P = 128
+N_FFT = 1024
+STRIDE = 1025
+NPAIR = 8
+NCHUNK = 4
+TXPOS = 1
+
+
+def tile_dftlayer_kernel(tc, x_bytes, x_scale, wsin, wcos, out_0, out_1):
+    nc = tc.nc
+    xb_view = x_bytes.rearrange("o b (t s) -> t (o b) s", s=STRIDE)
+    sc_view = x_scale.rearrange("o i (t s) -> (o i t) s", s=STRIDE)
+    w_views = [
+        wcos.rearrange("(c r p) n -> c p r n", c=2, r=4, p=P),
+        wsin.rearrange("(c r p) n -> c p r n", c=2, r=4, p=P),
+    ]
+    outs = [out_0, out_1]
+
+    with ExitStack() as ctx:
+        const = ctx.enter_context(tc.tile_pool(name="const", bufs=1))
+        keep = ctx.enter_context(tc.tile_pool(name="keep", bufs=1))
+        xbf_pool = ctx.enter_context(tc.tile_pool(name="xbf", bufs=3))
+        xpm_pool = ctx.enter_context(tc.tile_pool(name="xpm", bufs=3))
+        gw_pool = ctx.enter_context(tc.tile_pool(name="gw", bufs=2))
+        gx_pool = ctx.enter_context(tc.tile_pool(name="gx", bufs=3))
+        xq_pool = ctx.enter_context(tc.tile_pool(name="xq", bufs=3))
+        o_pool = ctx.enter_context(tc.tile_pool(name="o", bufs=8))
+        ps_pool = ctx.enter_context(tc.psum_pool(name="ps", bufs=8))
+        ctx.enter_context(tc.manual_schedule())
+
+        wraw = {}
+
+        def load_w(c, pieces):
+            src = w_views[c // 2][c % 2]
+            r0 = 0
+            for n in pieces:
+                t = keep.tile([P, n, N_FFT], BF16, name="wraw%d_%d" % (c, r0))
+                nc.sync.dma_start(out=t[:], in_=src[:, r0 : r0 + n, :])
+                for r in range(n):
+                    wraw[(c, r0 + r)] = t[:, r, :]
+                r0 += n
+
+        xsrc = {}
+
+        def load_x(b0, n):
+            t = keep.tile([P, n, N_FFT], U8, name="xbytes%d" % b0)
+            nc.sync.dma_start(out=t[:], in_=xb_view[:, b0 : b0 + n, 0:N_FFT])
+            for k in range(n):
+                xsrc[b0 + k] = t[:, k, :]
+
+        load_w(0, [1, 1, 1, 1])
+        scale_sb = const.tile([P, N_FFT], F32, name="scale_sb")
+        nc.sync.dma_start(out=scale_sb[:], in_=sc_view[:, 0:N_FFT])
+        load_x(0, 2)
+        load_w(1, [2, 2])
+        load_w(2, [2, 2])
+        load_x(2, 2)
+        load_w(3, [2, 1, 1])
+        load_x(4, 4)
+        load_x(8, 4)
+        load_x(12, 4)
+
+        ident = const.tile([P, P], F32, name="ident")
+        make_identity(nc, ident[:])
+        warm = const.tile([P, 2], F32, name="warm")
+        nc.vector.memset(warm[:, 0:1], 0.0)
+        nc.scalar.activation(out=warm[:, 1:2], in_=warm[:, 0:1], func=COPY, scale=-1.0)
+
+        wcodes = []
+        wscales = []
+        for c in range(NCHUNK):
+            wcodes.append(keep.tile([P, 2 * 512], U32, name="wcodes%d" % c, align_bytes=64))
+            wscales.append(keep.tile([P, 2 * 512], U8, name="wscales%d" % c, align_bytes=64))
+
+        state = {}
+
+        def transposes(words, ordered):
+            bank = ps_pool.tile([P, 512], F32, name="bank")
+            for g in range(2):
+                for u in range(2):
+                    if ordered:
+                        src = words[:, (2 * g + u) * P : (2 * g + u + 1) * P]
+                    else:
+                        src = words[:, 256 * g + u : 256 * (g + 1) : 2]
+                    nc.tensor.transpose(bank[:, (2 * g + u) * P : (2 * g + u + 1) * P], src, ident[:])
+            return bank
+
+        def empty_bank(eng, bank, dst):
+            src = bank[:].rearrange("p (g u r) -> p g r u", g=2, u=2)
+            if eng == "s":
+                nc.scalar.copy(out=dst.bitcast(F32), in_=src)
+            else:
+                nc.vector.tensor_copy(out=dst.bitcast(F32), in_=src)
+
+        def tw(c):
+            state[("wb", c)] = [transposes(wraw[(c, r)].bitcast(F32), False) for r in range(4)]
+
+        def ew(c, engs="ssss"):
+            gw = gw_pool.tile([P, 2, 4, P, 4], BF16, name="gw", align_bytes=64)
+            for r in range(4):
+                empty_bank(engs[r], state[("wb", c)][r], gw[:, :, r, :, :])
+            state[("gw", c)] = gw
+
+        def qw(c):
+            gw = state[("gw", c)]
+            nc.vector.quantize_mx(
+                out=wcodes[c][:].bitcast(FP8X4),
+                scales=wscales[c][:],
+                in_=gw[:].rearrange("p g r n t -> p (g r n t)"),
+            )
+
+        def prod(j, h):
+            if h == 0:
+                state[("xbf", j)] = xbf_pool.tile([P, 2, N_FFT], BF16, name="xbf")
+            xbf = state[("xbf", j)]
+            nc.vector.tensor_tensor(out=xbf[:, h, :], in0=xsrc[2 * j + h].bitcast(FP8), in1=scale_sb[:], op=MULT)
+
+        def rx(j):
+            xbf = state[("xbf", j)]
+            xpm = xpm_pool.tile([P, 2 * 512], F32, name="xpm")
+            nc.vector.tensor_copy(
+                out=xpm[:].rearrange("p (a u i) -> p a u i", a=4, u=2),
+                in_=xbf[:].rearrange("p h n -> p (h n)").bitcast(F32).rearrange("p (a i u) -> p a u i", a=4, u=2),
+            )
+            state[("xpm", j)] = xpm
+
+        def tx(j):
+            if ("xpm", j) in state:
+                xpm = state[("xpm", j)]
+                state[("xb", j)] = [transposes(xpm[:, h * 512 : (h + 1) * 512], True) for h in range(2)]
+            else:
+                xbf = state[("xbf", j)]
+                state[("xb", j)] = [transposes(xbf[:, h, :].bitcast(F32), False) for h in range(2)]
+
+        def ex(j, engs="vv"):
+            gx = gx_pool.tile([P, 2, 2, P, 4], BF16, name="gx", align_bytes=64)
+            for h in range(2):
+                empty_bank(engs[h], state[("xb", j)][h], gx[:, h, :, :, :])
+            state[("gx", j)] = gx
+
+        def qx(j):
+            gx = state[("gx", j)]
+            xc = xq_pool.tile([P, 512], U32, name="xc", align_bytes=64)
+            xs = xq_pool.tile([P, 512], U8, name="xs", align_bytes=64)
+            nc.vector.quantize_mx(
+                out=xc[:].bitcast(FP8X4), scales=xs[:], in_=gx[:].rearrange("p h g n t -> p (h g n t)")
+            )
+            state[("xc", j)] = (xc, xs)
+
+        def mb(j, h, which, engs="ss", fine=False):
+            xc, xs = state[("xc", j)]
+            b = 2 * j + h
+            ot = o_pool.tile([P, N_FFT], F32, name="ot")
+            for half in range(2):
+                c = 2 * which + half
+                acc = ps_pool.tile([P, 512], F32, name="bank")
+                for g in range(2):
+                    cols = slice((2 * h + g) * P, (2 * h + g + 1) * P)
+                    wcols = slice(g * 512, (g + 1) * 512)
+                    nc.tensor.matmul_mx(
+                        out=acc[:],
+                        lhsT=xc[:, cols].bitcast(FP8X4),
+                        lhsT_scale=xs[:, cols],
+                        rhs=wcodes[c][:, wcols].bitcast(FP8X4),
+                        rhs_scale=wscales[c][:, wcols],
+                        start=(g == 0),
+                        stop=(g == 1),
+                    )
+                dst = ot[:, half * 512 : (half + 1) * 512]
+                if engs[half] == "s":
+                    if which == 0:
+                        nc.scalar.copy(out=dst, in_=acc[:])
+                    else:
+                        nc.scalar.activation(out=dst, in_=acc[:], func=COPY, scale=-1.0)
+                else:
+                    if which == 0:
+                        nc.vector.tensor_copy(out=dst, in_=acc[:])
+                    else:
+                        nc.vector.tensor_scalar(out=dst, in0=acc[:], scalar1=-1.0, scalar2=None, op0=MULT)
+                if fine:
+                    nc.sync.dma_start(out=outs[which][:, b, half * 512 : (half + 1) * 512], in_=dst)
+            if not fine:
+                nc.sync.dma_start(out=outs[which][:, b, :], in_=ot[:])
+
+        tw(0)
+        ew(0, "vvvv")
+        prod(0, 0)
+        prod(0, 1)
+        qw(0)
+        tw(1)
+        ew(1)
+        tx(0)
+        ex(0, "ss")
+        qw(1)
+        qx(0)
+        tw(2)
+        ew(2)
+        prod(1, 0)
+        qw(2)
+        tw(3)
+        ew(3)
+        prod(1, 1)
+        qw(3)
+        prod(2, 0)
+        blocks = [(0, 0), (1, 0), (0, 1), (1, 1)]
+        for j in range(NPAIR):
+            for i in range(4):
+                h, which = blocks[i]
+                if i == TXPOS and j + 1 < NPAIR:
+                    tx(j + 1)
+                if j == NPAIR - 1 or (j == NPAIR - 2 and i == 3):
+                    engs = "sv"
+                else:
+                    engs = "ss"
+                mb(j, h, which, engs, j == NPAIR - 1 and i == 3)
+                k = i - TXPOS
+                if k == 0:
+                    if j + 1 < NPAIR:
+                        ex(j + 1, "ss" if j == 0 else "vv")
+                    if j + 2 < NPAIR:
+                        prod(j + 2, 1)
+                if k == 1:
+                    if j + 1 < NPAIR:
+                        qx(j + 1)
+                    if j + 2 < NPAIR:
+                        rx(j + 2)
+                if k == 2 and j + 3 < NPAIR:
+                    prod(j + 3, 0)

@@ -40,7 +40,7 @@ def tile_dftlayer_kernel(tc, x_bytes, x_scale, wsin, wcos, out_0, out_1):
         gw_pool = ctx.enter_context(tc.tile_pool(name="gw", bufs=2))
         gx_pool = ctx.enter_context(tc.tile_pool(name="gx", bufs=3))
         xq_pool = ctx.enter_context(tc.tile_pool(name="xq", bufs=3))
-        o_pool = ctx.enter_context(tc.tile_pool(name="o", bufs=8))
+        o_pool = ctx.enter_context(tc.tile_pool(name="o", bufs=5))
         ps_pool = ctx.enter_context(tc.psum_pool(name="ps", bufs=8))
         ctx.enter_context(tc.manual_schedule())
 
@@ -166,7 +166,9 @@ def tile_dftlayer_kernel(tc, x_bytes, x_scale, wsin, wcos, out_0, out_1):
         def mb(j, h, which, engs="ss", fine=False):
             xc, xs = state[("xc", j)]
             b = 2 * j + h
-            ot = o_pool.tile([P, N_FFT], F32, name="ot")
+            if h == 0:
+                state[("ot", j, which)] = o_pool.tile([P, 2, N_FFT], F32, name="ot")
+            ot = state[("ot", j, which)][:, h, :]
             for half in range(2):
                 c = 2 * which + half
                 acc = ps_pool.tile([P, 512], F32, name="bank")
@@ -195,8 +197,11 @@ def tile_dftlayer_kernel(tc, x_bytes, x_scale, wsin, wcos, out_0, out_1):
                         nc.vector.tensor_scalar(out=dst, in0=acc[:], scalar1=-1.0, scalar2=None, op0=MULT)
                 if fine:
                     nc.sync.dma_start(out=outs[which][:, b, half * 512 : (half + 1) * 512], in_=dst)
-            if not fine:
-                nc.sync.dma_start(out=outs[which][:, b, :], in_=ot[:])
+            if j == NPAIR - 1:
+                if not fine:
+                    nc.sync.dma_start(out=outs[which][:, b, :], in_=ot)
+            elif h == 1:
+                nc.sync.dma_start(out=outs[which][:, b - 1 : b + 1, :], in_=state[("ot", j, which)][:])
 
         tw(0)
         ew(0, "vvvv")

@@ -197,7 +197,7 @@ def tile_dftlayer_kernel(tc, x_bytes, x_scale, wsin, wcos, out_0, out_1):
                         nc.vector.tensor_scalar(out=dst, in0=acc[:], scalar1=-1.0, scalar2=None, op0=MULT)
                 if fine:
                     nc.sync.dma_start(out=outs[which][:, b, half * 512 : (half + 1) * 512], in_=dst)
-            if j == NPAIR - 1:
+            if j >= NPAIR - 2:
                 if not fine:
                     nc.sync.dma_start(out=outs[which][:, b, :], in_=ot)
             elif h == 1:

@@ -27,8 +27,8 @@ def tile_dftlayer_kernel(tc, x_bytes, x_scale, wsin, wcos, out_0, out_1):
     xb_view = x_bytes.rearrange("o b (t s) -> t (o b) s", s=STRIDE)
     sc_view = x_scale.rearrange("o i (t s) -> (o i t) s", s=STRIDE)
     w_views = [
-        wcos.rearrange("(c r p) n -> c p r n", c=2, r=4, p=P),
-        wsin.rearrange("(c r p) n -> c p r n", c=2, r=4, p=P),
+        wcos.rearrange("(c p r) n -> c p r n", c=2, r=4, p=P),
+        wsin.rearrange("(c p r) n -> c p r n", c=2, r=4, p=P),
     ]
     outs = [out_0, out_1]
 
@@ -64,14 +64,14 @@ def tile_dftlayer_kernel(tc, x_bytes, x_scale, wsin, wcos, out_0, out_1):
             for k in range(n):
                 xsrc[b0 + k] = t[:, k, :]
 
-        load_w(0, [1, 1, 1, 1])
+        load_w(0, [2, 2])
         scale_sb = const.tile([P, N_FFT], F32, name="scale_sb")
         nc.sync.dma_start(out=scale_sb[:], in_=sc_view[:, 0:N_FFT])
         load_x(0, 2)
         load_w(1, [2, 2])
         load_w(2, [2, 2])
         load_x(2, 2)
-        load_w(3, [2, 1, 1])
+        load_w(3, [2, 2])
         load_x(4, 4)
         load_x(8, 4)
         load_x(12, 4)
@@ -109,12 +109,29 @@ def tile_dftlayer_kernel(tc, x_bytes, x_scale, wsin, wcos, out_0, out_1):
                 nc.vector.tensor_copy(out=dst.bitcast(F32), in_=src)
 
         def tw(c):
-            state[("wb", c)] = [transposes(wraw[(c, r)].bitcast(F32), False) for r in range(4)]
+            banks = []
+            for a in range(2):
+                for g in range(2):
+                    bank = ps_pool.tile([P, 512], F32, name="bank")
+                    for b in range(2):
+                        words = wraw[(c, 2 * a + b)].bitcast(F32)
+                        for u in range(2):
+                            nc.tensor.transpose(
+                                bank[:, (2 * b + u) * P : (2 * b + u + 1) * P], words[:, 256 * g + u : 256 * (g + 1) : 2], ident[:]
+                            )
+                    banks.append(bank)
+            state[("wb", c)] = banks
 
         def ew(c, engs="ssss"):
-            gw = gw_pool.tile([P, 2, 4, P, 4], BF16, name="gw", align_bytes=64)
-            for r in range(4):
-                empty_bank(engs[r], state[("wb", c)][r], gw[:, :, r, :, :])
+            gw = gw_pool.tile([P, 2, P, 2, 2, 4], BF16, name="gw", align_bytes=64)
+            for a in range(2):
+                for g in range(2):
+                    src = state[("wb", c)][2 * a + g][:].rearrange("p (b u q) -> p q b u", b=2, u=2)
+                    dst = gw[:, g, :, a, :, :].bitcast(F32)
+                    if engs[2 * a + g] == "s":
+                        nc.scalar.copy(out=dst, in_=src)
+                    else:
+                        nc.vector.tensor_copy(out=dst, in_=src)
             state[("gw", c)] = gw
 
         def qw(c):
@@ -122,7 +139,7 @@ def tile_dftlayer_kernel(tc, x_bytes, x_scale, wsin, wcos, out_0, out_1):
             nc.vector.quantize_mx(
                 out=wcodes[c][:].bitcast(FP8X4),
                 scales=wscales[c][:],
-                in_=gw[:].rearrange("p g r n t -> p (g r n t)"),
+                in_=gw[:].rearrange("p g q a b t -> p (g q a b t)"),
             )
 
         def prod(j, h):

@@ -246,7 +246,7 @@ def tile_dftlayer_kernel(tc, x_bytes, x_scale, wsin, wcos, out_0, out_1):
                 h, which = blocks[i]
                 if i == TXPOS and j + 1 < NPAIR:
                     tx(j + 1)
-                if j == NPAIR - 1 or (j == NPAIR - 2 and i == 3):
+                if j == NPAIR - 1 or (j >= 1 and i == 3):
                     engs = "sv"
                 else:
                     engs = "ss"

@@ -246,6 +246,8 @@ def tile_dftlayer_kernel(tc, x_bytes, x_scale, wsin, wcos, out_0, out_1):
                 h, which = blocks[i]
                 if i == TXPOS and j + 1 < NPAIR:
                     tx(j + 1)
+                    if j == 0:
+                        ex(1, "ss")
                 if j == NPAIR - 1 or (j >= 1 and i == 3):
                     engs = "sv"
                 else:
@@ -253,8 +255,8 @@ def tile_dftlayer_kernel(tc, x_bytes, x_scale, wsin, wcos, out_0, out_1):
                 mb(j, h, which, engs, j == NPAIR - 1 and i == 3)
                 k = i - TXPOS
                 if k == 0:
-                    if j + 1 < NPAIR:
-                        ex(j + 1, "ss" if j == 0 else "vv")
+                    if 0 < j < NPAIR - 1:
+                        ex(j + 1, "vv")
                     if j + 2 < NPAIR:
                         prod(j + 2, 1)
                 if k == 1:

@@ -46,15 +46,12 @@ def tile_dftlayer_kernel(tc, x_bytes, x_scale, wsin, wcos, out_0, out_1):
 
         wraw = {}
 
-        def load_w(c, pieces):
+        def load_w(c, a):
             src = w_views[c // 2][c % 2]
-            r0 = 0
-            for n in pieces:
-                t = keep.tile([P, n, N_FFT], BF16, name="wraw%d_%d" % (c, r0))
-                nc.sync.dma_start(out=t[:], in_=src[:, r0 : r0 + n, :])
-                for r in range(n):
-                    wraw[(c, r0 + r)] = t[:, r, :]
-                r0 += n
+            t = keep.tile([P, 2, N_FFT], BF16, name="wraw%d_%d" % (c, a))
+            nc.sync.dma_start(out=t[:], in_=src[:, 2 * a : 2 * a + 2, :])
+            for r in range(2):
+                wraw[(c, 2 * a + r)] = t[:, r, :]
 
         xsrc = {}
 
@@ -64,14 +61,18 @@ def tile_dftlayer_kernel(tc, x_bytes, x_scale, wsin, wcos, out_0, out_1):
             for k in range(n):
                 xsrc[b0 + k] = t[:, k, :]
 
-        load_w(0, [2, 2])
         scale_sb = const.tile([P, N_FFT], F32, name="scale_sb")
         nc.sync.dma_start(out=scale_sb[:], in_=sc_view[:, 0:N_FFT])
         load_x(0, 2)
-        load_w(1, [2, 2])
-        load_w(2, [2, 2])
+        load_w(0, 0)
         load_x(2, 2)
-        load_w(3, [2, 2])
+        load_w(0, 1)
+        load_w(1, 0)
+        load_w(1, 1)
+        load_w(2, 0)
+        load_w(2, 1)
+        load_w(3, 0)
+        load_w(3, 1)
         load_x(4, 4)
         load_x(8, 4)
         load_x(12, 4)
@@ -108,31 +109,30 @@ def tile_dftlayer_kernel(tc, x_bytes, x_scale, wsin, wcos, out_0, out_1):
             else:
                 nc.vector.tensor_copy(out=dst.bitcast(F32), in_=src)
 
-        def tw(c):
+        def tw(c, a):
             banks = []
-            for a in range(2):
-                for g in range(2):
-                    bank = ps_pool.tile([P, 512], F32, name="bank")
-                    for b in range(2):
-                        words = wraw[(c, 2 * a + b)].bitcast(F32)
-                        for u in range(2):
-                            nc.tensor.transpose(
-                                bank[:, (2 * b + u) * P : (2 * b + u + 1) * P], words[:, 256 * g + u : 256 * (g + 1) : 2], ident[:]
-                            )
-                    banks.append(bank)
-            state[("wb", c)] = banks
+            for g in range(2):
+                bank = ps_pool.tile([P, 512], F32, name="bank")
+                for b in range(2):
+                    words = wraw[(c, 2 * a + b)].bitcast(F32)
+                    for u in range(2):
+                        nc.tensor.transpose(
+                            bank[:, (2 * b + u) * P : (2 * b + u + 1) * P], words[:, 256 * g + u : 256 * (g + 1) : 2], ident[:]
+                        )
+                banks.append(bank)
+            state[("wb", c, a)] = banks
 
-        def ew(c, engs="ssss"):
-            gw = gw_pool.tile([P, 2, P, 2, 2, 4], BF16, name="gw", align_bytes=64)
-            for a in range(2):
-                for g in range(2):
-                    src = state[("wb", c)][2 * a + g][:].rearrange("p (b u q) -> p q b u", b=2, u=2)
-                    dst = gw[:, g, :, a, :, :].bitcast(F32)
-                    if engs[2 * a + g] == "s":
-                        nc.scalar.copy(out=dst, in_=src)
-                    else:
-                        nc.vector.tensor_copy(out=dst, in_=src)
-            state[("gw", c)] = gw
+        def ew(c, a, engs="ss"):
+            if a == 0:
+                state[("gw", c)] = gw_pool.tile([P, 2, P, 2, 2, 4], BF16, name="gw", align_bytes=64)
+            gw = state[("gw", c)]
+            for g in range(2):
+                src = state[("wb", c, a)][g][:].rearrange("p (b u q) -> p q b u", b=2, u=2)
+                dst = gw[:, g, :, a, :, :].bitcast(F32)
+                if engs[g] == "s":
+                    nc.scalar.copy(out=dst, in_=src)
+                else:
+                    nc.vector.tensor_copy(out=dst, in_=src)
 
         def qw(c):
             gw = state[("gw", c)]
@@ -171,6 +171,15 @@ def tile_dftlayer_kernel(tc, x_bytes, x_scale, wsin, wcos, out_0, out_1):
                 empty_bank(engs[h], state[("xb", j)][h], gx[:, h, :, :, :])
             state[("gx", j)] = gx
 
+        def txh(j, h):
+            xbf = state[("xbf", j)]
+            state[("xbh", j, h)] = transposes(xbf[:, h, :].bitcast(F32), False)
+
+        def exh(j, h, eng):
+            if h == 0:
+                state[("gx", j)] = gx_pool.tile([P, 2, 2, P, 4], BF16, name="gx", align_bytes=64)
+            empty_bank(eng, state[("xbh", j, h)], state[("gx", j)][:, h, :, :, :])
+
         def qx(j):
             gx = state[("gx", j)]
             xc = xq_pool.tile([P, 512], U32, name="xc", align_bytes=64)
@@ -180,82 +189,119 @@ def tile_dftlayer_kernel(tc, x_bytes, x_scale, wsin, wcos, out_0, out_1):
             )
             state[("xc", j)] = (xc, xs)
 
-        def mb(j, h, which, engs="ss", fine=False):
+        def bank_of(j, h, c, eng):
             xc, xs = state[("xc", j)]
-            b = 2 * j + h
-            if h == 0:
+            which = c // 2
+            half = c % 2
+            if ("ot", j, which) not in state:
                 state[("ot", j, which)] = o_pool.tile([P, 2, N_FFT], F32, name="ot")
-            ot = state[("ot", j, which)][:, h, :]
-            for half in range(2):
-                c = 2 * which + half
-                acc = ps_pool.tile([P, 512], F32, name="bank")
-                for g in range(2):
-                    cols = slice((2 * h + g) * P, (2 * h + g + 1) * P)
-                    wcols = slice(g * 512, (g + 1) * 512)
-                    nc.tensor.matmul_mx(
-                        out=acc[:],
-                        lhsT=xc[:, cols].bitcast(FP8X4),
-                        lhsT_scale=xs[:, cols],
-                        rhs=wcodes[c][:, wcols].bitcast(FP8X4),
-                        rhs_scale=wscales[c][:, wcols],
-                        start=(g == 0),
-                        stop=(g == 1),
-                    )
-                dst = ot[:, half * 512 : (half + 1) * 512]
-                if engs[half] == "s":
-                    if which == 0:
-                        nc.scalar.copy(out=dst, in_=acc[:])
-                    else:
-                        nc.scalar.activation(out=dst, in_=acc[:], func=COPY, scale=-1.0)
+            acc = ps_pool.tile([P, 512], F32, name="bank")
+            for g in range(2):
+                cols = slice((2 * h + g) * P, (2 * h + g + 1) * P)
+                wcols = slice(g * 512, (g + 1) * 512)
+                nc.tensor.matmul_mx(
+                    out=acc[:],
+                    lhsT=xc[:, cols].bitcast(FP8X4),
+                    lhsT_scale=xs[:, cols],
+                    rhs=wcodes[c][:, wcols].bitcast(FP8X4),
+                    rhs_scale=wscales[c][:, wcols],
+                    start=(g == 0),
+                    stop=(g == 1),
+                )
+            dst = state[("ot", j, which)][:, h, half * 512 : (half + 1) * 512]
+            if eng == "s":
+                if which == 0:
+                    nc.scalar.copy(out=dst, in_=acc[:])
                 else:
-                    if which == 0:
-                        nc.vector.tensor_copy(out=dst, in_=acc[:])
-                    else:
-                        nc.vector.tensor_scalar(out=dst, in0=acc[:], scalar1=-1.0, scalar2=None, op0=MULT)
+                    nc.scalar.activation(out=dst, in_=acc[:], func=COPY, scale=-1.0)
+            else:
+                if which == 0:
+                    nc.vector.tensor_copy(out=dst, in_=acc[:])
+                else:
+                    nc.vector.tensor_scalar(out=dst, in0=acc[:], scalar1=-1.0, scalar2=None, op0=MULT)
+            return dst
+
+        def store_pair(j, which):
+            nc.sync.dma_start(out=outs[which][:, 2 * j : 2 * j + 2, :], in_=state[("ot", j, which)][:])
+
+        def mb(j, h, which, engs="ss", fine=False):
+            b = 2 * j + h
+            for half in range(2):
+                dst = bank_of(j, h, 2 * which + half, engs[half])
                 if fine:
                     nc.sync.dma_start(out=outs[which][:, b, half * 512 : (half + 1) * 512], in_=dst)
             if j >= NPAIR - 2:
                 if not fine:
-                    nc.sync.dma_start(out=outs[which][:, b, :], in_=ot)
+                    nc.sync.dma_start(out=outs[which][:, b, :], in_=state[("ot", j, which)][:, h, :])
             elif h == 1:
-                nc.sync.dma_start(out=outs[which][:, b - 1 : b + 1, :], in_=state[("ot", j, which)][:])
+                store_pair(j, which)
 
-        tw(0)
-        ew(0, "vvvv")
         prod(0, 0)
         prod(0, 1)
-        qw(0)
-        tw(1)
-        ew(1)
-        tx(0)
-        ex(0, "ss")
-        qw(1)
-        qx(0)
-        tw(2)
-        ew(2)
         prod(1, 0)
-        qw(2)
-        tw(3)
-        ew(3)
         prod(1, 1)
+        txh(0, 0)
+        exh(0, 0, "s")
+        tw(0, 0)
+        ew(0, 0, "ss")
+        txh(0, 1)
+        exh(0, 1, "s")
+        tw(0, 1)
+        ew(0, 1, "ss")
+        txh(1, 0)
+        exh(1, 0, "s")
+        qx(0)
+        tw(1, 0)
+        ew(1, 0, "ss")
+        txh(1, 1)
+        exh(1, 1, "v")
+        qw(0)
+        qx(1)
+        tw(1, 1)
+        ew(1, 1, "ss")
+        qw(1)
+        tw(2, 0)
+        ew(2, 0, "ss")
+        tw(2, 1)
+        ew(2, 1, "ss")
+        tw(3, 0)
+        ew(3, 0, "vv")
+        qw(2)
+        tw(3, 1)
+        ew(3, 1, "ss")
         qw(3)
         prod(2, 0)
+        mb(0, 0, 0)
+        mb(0, 1, 0)
+        prod(2, 1)
+        mb(1, 0, 0)
+        rx(2)
+        mb(1, 1, 0)
+        prod(3, 0)
+        mb(0, 0, 1)
+        tx(2)
+        ex(2, "vv")
+        mb(0, 1, 1)
+        prod(3, 1)
+        qx(2)
+        mb(1, 0, 1)
+        rx(3)
+        mb(1, 1, 1)
+        prod(4, 0)
         blocks = [(0, 0), (1, 0), (0, 1), (1, 1)]
-        for j in range(NPAIR):
+        for j in range(2, NPAIR):
             for i in range(4):
                 h, which = blocks[i]
                 if i == TXPOS and j + 1 < NPAIR:
                     tx(j + 1)
-                    if j == 0:
-                        ex(1, "ss")
-                if j == NPAIR - 1 or (j >= 1 and i == 3):
+                if j == NPAIR - 1 or i == 3:
                     engs = "sv"
                 else:
                     engs = "ss"
                 mb(j, h, which, engs, j == NPAIR - 1 and i == 3)
                 k = i - TXPOS
                 if k == 0:
-                    if 0 < j < NPAIR - 1:
+                    if j < NPAIR - 1:
                         ex(j + 1, "vv")
                     if j + 2 < NPAIR:
                         prod(j + 2, 1)

@@ -62,8 +62,10 @@ def tile_dftlayer_kernel(tc, x_bytes, x_scale, wsin, wcos, out_0, out_1):
                 xsrc[b0 + k] = t[:, k, :]
 
         scale_sb = const.tile([P, N_FFT], F32, name="scale_sb")
-        nc.sync.dma_start(out=scale_sb[:], in_=sc_view[:, 0:N_FFT])
-        load_x(0, 2)
+        nc.sync.dma_start(out=scale_sb[:, 0:512], in_=sc_view[:, 0:512])
+        load_x(0, 1)
+        nc.sync.dma_start(out=scale_sb[:, 512:N_FFT], in_=sc_view[:, 512:N_FFT])
+        load_x(1, 1)
         load_w(0, 0)
         load_x(2, 2)
         load_w(0, 1)
@@ -180,6 +182,23 @@ def tile_dftlayer_kernel(tc, x_bytes, x_scale, wsin, wcos, out_0, out_1):
                 state[("gx", j)] = gx_pool.tile([P, 2, 2, P, 4], BF16, name="gx", align_bytes=64)
             empty_bank(eng, state[("xbh", j, h)], state[("gx", j)][:, h, :, :, :])
 
+        def prodh(j, h, g):
+            if h == 0 and g == 0:
+                state[("xbf", j)] = xbf_pool.tile([P, 2, N_FFT], BF16, name="xbf")
+            cols = slice(512 * g, 512 * (g + 1))
+            nc.vector.tensor_tensor(
+                out=state[("xbf", j)][:, h, cols], in0=xsrc[2 * j + h][:, cols].bitcast(FP8), in1=scale_sb[:, cols], op=MULT
+            )
+
+        def txhg(j, h, g):
+            if g == 0:
+                bank = ps_pool.tile([P, 512], F32, name="bank")
+                state[("xbh", j, h)] = bank
+            bank = state[("xbh", j, h)]
+            words = state[("xbf", j)][:, h, :].bitcast(F32)
+            for u in range(2):
+                nc.tensor.transpose(bank[:, (2 * g + u) * P : (2 * g + u + 1) * P], words[:, 256 * g + u : 256 * (g + 1) : 2], ident[:])
+
         def qx(j):
             gx = state[("gx", j)]
             xc = xq_pool.tile([P, 512], U32, name="xc", align_bytes=64)
@@ -236,15 +255,19 @@ def tile_dftlayer_kernel(tc, x_bytes, x_scale, wsin, wcos, out_0, out_1):
             elif h == 1:
                 store_pair(j, which)
 
-        prod(0, 0)
-        prod(0, 1)
+        prodh(0, 0, 0)
+        prodh(0, 0, 1)
+        prodh(0, 1, 0)
+        prodh(0, 1, 1)
         prod(1, 0)
         prod(1, 1)
-        txh(0, 0)
+        txhg(0, 0, 0)
+        txhg(0, 0, 1)
         exh(0, 0, "s")
+        txhg(0, 1, 0)
         tw(0, 0)
         ew(0, 0, "ss")
-        txh(0, 1)
+        txhg(0, 1, 1)
         exh(0, 1, "s")
         tw(0, 1)
         ew(0, 1, "ss")

from contextlib import ExitStack

import concourse.mybir as mybir
from concourse.masks import make_identity

FLOPS = 2 * 2048 * 1024 * 2048

F32 = mybir.dt.float32
BF16 = mybir.dt.bfloat16
U32 = mybir.dt.uint32
U8 = mybir.dt.uint8
FP8 = mybir.dt.float8_e4m3fn
FP8X4 = mybir.dt.float8_e4m3fn_x4
MULT = mybir.AluOpType.mult
COPY = mybir.ActivationFunctionType.Copy

P = 128
N_FFT = 1024
STRIDE = 1025
NPAIR = 8
NCHUNK = 4
TXPOS = 1


def tile_dftlayer_kernel(tc, x_bytes, x_scale, wsin, wcos, out_0, out_1):
    nc = tc.nc
    xb_view = x_bytes.rearrange("o b (t s) -> t (o b) s", s=STRIDE)
    sc_view = x_scale.rearrange("o i (t s) -> (o i t) s", s=STRIDE)
    w_views = [
        wcos.rearrange("(c p r) n -> c p r n", c=2, r=4, p=P),
        wsin.rearrange("(c p r) n -> c p r n", c=2, r=4, p=P),
    ]
    outs = [out_0, out_1]

    with ExitStack() as ctx:
        const = ctx.enter_context(tc.tile_pool(name="const", bufs=1))
        keep = ctx.enter_context(tc.tile_pool(name="keep", bufs=1))
        xbf_pool = ctx.enter_context(tc.tile_pool(name="xbf", bufs=3))
        xpm_pool = ctx.enter_context(tc.tile_pool(name="xpm", bufs=3))
        gw_pool = ctx.enter_context(tc.tile_pool(name="gw", bufs=2))
        gx_pool = ctx.enter_context(tc.tile_pool(name="gx", bufs=3))
        xq_pool = ctx.enter_context(tc.tile_pool(name="xq", bufs=3))
        o_pool = ctx.enter_context(tc.tile_pool(name="o", bufs=5))
        ps_pool = ctx.enter_context(tc.psum_pool(name="ps", bufs=8))
        ctx.enter_context(tc.manual_schedule())

        wraw = {}

        def load_w(c, a):
            src = w_views[c // 2][c % 2]
            t = keep.tile([P, 2, N_FFT], BF16, name="wraw%d_%d" % (c, a))
            nc.sync.dma_start(out=t[:], in_=src[:, 2 * a : 2 * a + 2, :])
            for r in range(2):
                wraw[(c, 2 * a + r)] = t[:, r, :]

        xsrc = {}

        def load_x(b0, n):
            t = keep.tile([P, n, N_FFT], U8, name="xbytes%d" % b0)
            nc.sync.dma_start(out=t[:], in_=xb_view[:, b0 : b0 + n, 0:N_FFT])
            for k in range(n):
                xsrc[b0 + k] = t[:, k, :]

        scale_sb = const.tile([P, N_FFT], F32, name="scale_sb")
        nc.sync.dma_start(out=scale_sb[:, 0:512], in_=sc_view[:, 0:512])
        load_x(0, 1)
        nc.sync.dma_start(out=scale_sb[:, 512:N_FFT], in_=sc_view[:, 512:N_FFT])
        load_x(1, 1)
        load_w(0, 0)
        load_x(2, 2)
        load_w(0, 1)
        load_w(1, 0)
        load_w(1, 1)
        load_w(2, 0)
        load_w(2, 1)
        load_w(3, 0)
        load_w(3, 1)
        load_x(4, 4)
        load_x(8, 4)
        load_x(12, 4)

        ident = const.tile([P, P], F32, name="ident")
        make_identity(nc, ident[:])
        warm = const.tile([P, 2], F32, name="warm")
        nc.vector.memset(warm[:, 0:1], 0.0)
        nc.scalar.activation(out=warm[:, 1:2], in_=warm[:, 0:1], func=COPY, scale=-1.0)

        wcodes = []
        wscales = []
        for c in range(NCHUNK):
            wcodes.append(keep.tile([P, 2 * 512], U32, name="wcodes%d" % c, align_bytes=64))
            wscales.append(keep.tile([P, 2 * 512], U8, name="wscales%d" % c, align_bytes=64))

        state = {}

        def transposes(words, ordered):
            bank = ps_pool.tile([P, 512], F32, name="bank")
            for g in range(2):
                for u in range(2):
                    if ordered:
                        src = words[:, (2 * g + u) * P : (2 * g + u + 1) * P]
                    else:
                        src = words[:, 256 * g + u : 256 * (g + 1) : 2]
                    nc.tensor.transpose(bank[:, (2 * g + u) * P : (2 * g + u + 1) * P], src, ident[:])
            return bank

        def empty_bank(eng, bank, dst):
            src = bank[:].rearrange("p (g u r) -> p g r u", g=2, u=2)
            if eng == "s":
                nc.scalar.copy(out=dst.bitcast(F32), in_=src)
            else:
                nc.vector.tensor_copy(out=dst.bitcast(F32), in_=src)

        def tw(c, a):
            banks = []
            for g in range(2):
                bank = ps_pool.tile([P, 512], F32, name="bank")
                for b in range(2):
                    words = wraw[(c, 2 * a + b)].bitcast(F32)
                    for u in range(2):
                        nc.tensor.transpose(
                            bank[:, (2 * b + u) * P : (2 * b + u + 1) * P], words[:, 256 * g + u : 256 * (g + 1) : 2], ident[:]
                        )
                banks.append(bank)
            state[("wb", c, a)] = banks

        def ew(c, a, engs="ss"):
            if a == 0:
                state[("gw", c)] = gw_pool.tile([P, 2, P, 2, 2, 4], BF16, name="gw", align_bytes=64)
            gw = state[("gw", c)]
            for g in range(2):
                src = state[("wb", c, a)][g][:].rearrange("p (b u q) -> p q b u", b=2, u=2)
                dst = gw[:, g, :, a, :, :].bitcast(F32)
                if engs[g] == "s":
                    nc.scalar.copy(out=dst, in_=src)
                else:
                    nc.vector.tensor_copy(out=dst, in_=src)

        def qw(c):
            gw = state[("gw", c)]
            nc.vector.quantize_mx(
                out=wcodes[c][:].bitcast(FP8X4),
                scales=wscales[c][:],
                in_=gw[:].rearrange("p g q a b t -> p (g q a b t)"),
            )

        def prod(j, h):
            if h == 0:
                state[("xbf", j)] = xbf_pool.tile([P, 2, N_FFT], BF16, name="xbf")
            xbf = state[("xbf", j)]
            nc.vector.tensor_tensor(out=xbf[:, h, :], in0=xsrc[2 * j + h].bitcast(FP8), in1=scale_sb[:], op=MULT)

        def rx(j):
            xbf = state[("xbf", j)]
            xpm = xpm_pool.tile([P, 2 * 512], F32, name="xpm")
            nc.vector.tensor_copy(
                out=xpm[:].rearrange("p (a u i) -> p a u i", a=4, u=2),
                in_=xbf[:].rearrange("p h n -> p (h n)").bitcast(F32).rearrange("p (a i u) -> p a u i", a=4, u=2),
            )
            state[("xpm", j)] = xpm

        def tx(j):
            if ("xpm", j) in state:
                xpm = state[("xpm", j)]
                state[("xb", j)] = [transposes(xpm[:, h * 512 : (h + 1) * 512], True) for h in range(2)]
            else:
                xbf = state[("xbf", j)]
                state[("xb", j)] = [transposes(xbf[:, h, :].bitcast(F32), False) for h in range(2)]

        def ex(j, engs="vv"):
            gx = gx_pool.tile([P, 2, 2, P, 4], BF16, name="gx", align_bytes=64)
            for h in range(2):
                empty_bank(engs[h], state[("xb", j)][h], gx[:, h, :, :, :])
            state[("gx", j)] = gx

        def txh(j, h):
            xbf = state[("xbf", j)]
            state[("xbh", j, h)] = transposes(xbf[:, h, :].bitcast(F32), False)

        def exh(j, h, eng):
            if h == 0:
                state[("gx", j)] = gx_pool.tile([P, 2, 2, P, 4], BF16, name="gx", align_bytes=64)
            empty_bank(eng, state[("xbh", j, h)], state[("gx", j)][:, h, :, :, :])

        def prodh(j, h, g):
            if h == 0 and g == 0:
                state[("xbf", j)] = xbf_pool.tile([P, 2, N_FFT], BF16, name="xbf")
            cols = slice(512 * g, 512 * (g + 1))
            nc.vector.tensor_tensor(
                out=state[("xbf", j)][:, h, cols], in0=xsrc[2 * j + h][:, cols].bitcast(FP8), in1=scale_sb[:, cols], op=MULT
            )

        def txhg(j, h, g):
            if g == 0:
                bank = ps_pool.tile([P, 512], F32, name="bank")
                state[("xbh", j, h)] = bank
            bank = state[("xbh", j, h)]
            words = state[("xbf", j)][:, h, :].bitcast(F32)
            for u in range(2):
                nc.tensor.transpose(bank[:, (2 * g + u) * P : (2 * g + u + 1) * P], words[:, 256 * g + u : 256 * (g + 1) : 2], ident[:])

        def qx(j):
            gx = state[("gx", j)]
            xc = xq_pool.tile([P, 512], U32, name="xc", align_bytes=64)
            xs = xq_pool.tile([P, 512], U8, name="xs", align_bytes=64)
            nc.vector.quantize_mx(
                out=xc[:].bitcast(FP8X4), scales=xs[:], in_=gx[:].rearrange("p h g n t -> p (h g n t)")
            )
            state[("xc", j)] = (xc, xs)

        def bank_of(j, h, c, eng):
            xc, xs = state[("xc", j)]
            which = c // 2
            half = c % 2
            if ("ot", j, which) not in state:
                state[("ot", j, which)] = o_pool.tile([P, 2, N_FFT], F32, name="ot")
            acc = ps_pool.tile([P, 512], F32, name="bank")
            for g in range(2):
                cols = slice((2 * h + g) * P, (2 * h + g + 1) * P)
                wcols = slice(g * 512, (g + 1) * 512)
                nc.tensor.matmul_mx(
                    out=acc[:],
                    lhsT=xc[:, cols].bitcast(FP8X4),
                    lhsT_scale=xs[:, cols],
                    rhs=wcodes[c][:, wcols].bitcast(FP8X4),
                    rhs_scale=wscales[c][:, wcols],
                    start=(g == 0),
                    stop=(g == 1),
                )
            dst = state[("ot", j, which)][:, h, half * 512 : (half + 1) * 512]
            if eng == "s":
                if which == 0:
                    nc.scalar.copy(out=dst, in_=acc[:])
                else:
                    nc.scalar.activation(out=dst, in_=acc[:], func=COPY, scale=-1.0)
            else:
                if which == 0:
                    nc.vector.tensor_copy(out=dst, in_=acc[:])
                else:
                    nc.vector.tensor_scalar(out=dst, in0=acc[:], scalar1=-1.0, scalar2=None, op0=MULT)
            return dst

        def store_pair(j, which):
            nc.sync.dma_start(out=outs[which][:, 2 * j : 2 * j + 2, :], in_=state[("ot", j, which)][:])

        def mb(j, h, which, engs="ss", fine=False):
            b = 2 * j + h
            for half in range(2):
                dst = bank_of(j, h, 2 * which + half, engs[half])
                if fine:
                    nc.sync.dma_start(out=outs[which][:, b, half * 512 : (half + 1) * 512], in_=dst)
            if j >= NPAIR - 2:
                if not fine:
                    nc.sync.dma_start(out=outs[which][:, b, :], in_=state[("ot", j, which)][:, h, :])
            elif h == 1:
                store_pair(j, which)

        prodh(0, 0, 0)
        prodh(0, 0, 1)
        prodh(0, 1, 0)
        prodh(0, 1, 1)
        prod(1, 0)
        prod(1, 1)
        txhg(0, 0, 0)
        txhg(0, 0, 1)
        exh(0, 0, "s")
        txhg(0, 1, 0)
        tw(0, 0)
        ew(0, 0, "ss")
        txhg(0, 1, 1)
        exh(0, 1, "s")
        tw(0, 1)
        ew(0, 1, "ss")
        txh(1, 0)
        exh(1, 0, "s")
        qx(0)
        tw(1, 0)
        ew(1, 0, "ss")
        txh(1, 1)
        exh(1, 1, "v")
        qw(0)
        qx(1)
        tw(1, 1)
        ew(1, 1, "ss")
        qw(1)
        tw(2, 0)
        ew(2, 0, "ss")
        tw(2, 1)
        ew(2, 1, "ss")
        tw(3, 0)
        ew(3, 0, "vv")
        qw(2)
        tw(3, 1)
        ew(3, 1, "ss")
        qw(3)
        prod(2, 0)
        mb(0, 0, 0)
        mb(0, 1, 0)
        prod(2, 1)
        mb(1, 0, 0)
        rx(2)
        mb(1, 1, 0)
        prod(3, 0)
        mb(0, 0, 1)
        tx(2)
        ex(2, "vv")
        mb(0, 1, 1)
        prod(3, 1)
        qx(2)
        mb(1, 0, 1)
        rx(3)
        mb(1, 1, 1)
        prod(4, 0)
        blocks = [(0, 0), (1, 0), (0, 1), (1, 1)]
        for j in range(2, NPAIR):
            for i in range(4):
                h, which = blocks[i]
                if i == TXPOS and j + 1 < NPAIR:
                    tx(j + 1)
                if j == NPAIR - 1 or i == 3:
                    engs = "sv"
                else:
                    engs = "ss"
                mb(j, h, which, engs, j == NPAIR - 1 and i == 3)
                k = i - TXPOS
                if k == 0:
                    if j < NPAIR - 1:
                        ex(j + 1, "vv")
                    if j + 2 < NPAIR:
                        prod(j + 2, 1)
                if k == 1:
                    if j + 1 < NPAIR:
                        qx(j + 1)
                    if j + 2 < NPAIR:
                        rx(j + 2)
                if k == 2 and j + 3 < NPAIR:
                    prod(j + 3, 0)
